import numpy as np
import ml_dtypes


def mxq(x, axis, fmt="e4m3"):
    dtype, down = {"e4m3": (ml_dtypes.float8_e4m3fn, 7), "e5m2": (ml_dtypes.float8_e5m2, 14)}[fmt]
    v = np.moveaxis(np.asarray(x, np.float32).astype(ml_dtypes.bfloat16).astype(np.float64), axis, -1)
    blocks = v.reshape(v.shape[:-1] + (-1, 32))
    amax = np.abs(blocks).max(-1, keepdims=True)
    byte = np.maximum(np.where(amax > 0, np.frexp(amax)[1] - 1 + 127, 0) - down, 1)
    scale = np.exp2(byte - 127.0)
    codes = (blocks / scale).astype(np.float32).astype(dtype).astype(np.float64)
    return np.moveaxis((codes * scale).reshape(v.shape), -1, axis)


WIDE = False


def mx_kscale(k):
    if not WIDE:
        return np.ones(k)
    levels = np.array([10, -10, 5, -5, 0])
    a = np.random.permutation(np.resize(levels, k // 512 * 4)).reshape(k // 512, 4)
    idx = np.arange(k)
    return np.exp2(a[idx // 512, idx % 128 // 32])


BF16 = ml_dtypes.bfloat16


def bf(x):
    return np.asarray(x, np.float32).astype(BF16)


def f64(x):
    return np.asarray(x).astype(np.float64)


E2M1 = np.array([0.0, 0.5, 1.0, 1.5, 2.0, 3.0, 4.0, 6.0, -0.0, -0.5, -1.0, -1.5, -2.0, -3.0, -4.0, -6.0])


def pack_weight(w, fmt):
    k, n = w.shape
    w = f64(bf(w)).reshape(k // 32, 32, n)
    amax = np.abs(w).max(1)
    if fmt == "e4m3":
        byte = np.frexp(amax)[1] - 1 + 127 - 7
    else:
        mant, ex = np.frexp(amax / 6.0)
        byte = np.where(mant > 0.5, ex, ex - 1) + 127
    byte = np.clip(np.where(amax > 0, byte, 1), 1, 254)
    scaled = (w * np.exp2(127.0 - byte)[:, None, :]).reshape(k, n).astype(np.float32)
    by_word = np.ascontiguousarray(scaled.reshape(k // 512, 128, 4, n).transpose(0, 1, 3, 2))
    if fmt == "e4m3":
        words = by_word.astype(ml_dtypes.float8_e4m3fn).view(np.uint8)
    else:
        c = by_word.astype(ml_dtypes.float4_e2m1fn).view(np.uint8) & 0xF
        words = c[..., 0::2] | (c[..., 1::2] << 4)
    return np.ascontiguousarray(words), np.ascontiguousarray(byte.astype(np.uint8).reshape(k // 512, 16, n))


def unpack_weight(words, scales, fmt):
    g, p, n, _ = words.shape
    if fmt == "e4m3":
        vals = np.ascontiguousarray(words).view(ml_dtypes.float8_e4m3fn).astype(np.float64)
    else:
        nib = np.empty((g, p, n, 4), np.uint8)
        nib[..., 0::2] = words & 0xF
        nib[..., 1::2] = words >> 4
        vals = E2M1[nib]
    vals = vals * np.repeat(np.exp2(scales.astype(np.float64) - 127.0), 8, axis=1)[..., None]
    return vals.transpose(0, 1, 3, 2).reshape(g * 512, n)


B, S, HID, H, HKV, D, QB = 1, 512, 2048, 16, 8, 128, 512
HALF = D // 2
ROPE_BASE = 10000.0
FMT = "e4m3"


def rope_tables():
    inv_freq = 1.0 / (ROPE_BASE ** (np.arange(0, D, 2) / D))
    freqs = np.outer(np.arange(S), inv_freq)
    emb = np.concatenate([freqs, freqs], axis=-1)
    return np.cos(emb), np.sin(emb)


def rotate_half(t):
    return np.concatenate([-t[..., HALF:], t[..., :HALF]], axis=-1)


def apply_rope(t, cos, sin):
    return t * cos[None, None, :, :] + rotate_half(t) * sin[None, None, :, :]


def heads(y, n):
    return y.reshape(B, S, n, D).transpose(0, 2, 1, 3)


def setup_inputs():
    s = mx_kscale(HID)
    w = 1.0 / np.sqrt(HID)
    cos, sin = rope_tables()
    x = bf(np.random.standard_normal((B, S, HID)) * s)
    Wq_words, Wq_scales = pack_weight((np.random.standard_normal((H * D, HID)) * w / s[None, :]).T, FMT)
    Wk_words, Wk_scales = pack_weight((np.random.standard_normal((HKV * D, HID)) * w / s[None, :]).T, FMT)
    Wv_words, Wv_scales = pack_weight((np.random.standard_normal((HKV * D, HID)) * w / s[None, :]).T, FMT)
    return {"x": x,
            "Wq_words": Wq_words, "Wq_scales": Wq_scales,
            "Wk_words": Wk_words, "Wk_scales": Wk_scales,
            "Wv_words": Wv_words, "Wv_scales": Wv_scales,
            "cos": bf(cos), "sin": bf(sin)}


def reference(x, Wq_words, Wq_scales, Wk_words, Wk_scales, Wv_words, Wv_scales, cos, sin):
    xq = mxq(f64(x), 2, "e4m3")
    q = heads(xq @ unpack_weight(Wq_words, Wq_scales, FMT), H)
    k = heads(xq @ unpack_weight(Wk_words, Wk_scales, FMT), HKV)
    v = heads(xq @ unpack_weight(Wv_words, Wv_scales, FMT), HKV)
    c, sn = f64(cos), f64(sin)
    return apply_rope(q, c, sn), apply_rope(k, c, sn), v

@@ -1,0 +1,186 @@
+from contextlib import ExitStack
+
+import concourse.mybir as mybir
+from concourse.masks import make_identity
+
+F32 = mybir.dt.float32
+BF16 = mybir.dt.bfloat16
+I32 = mybir.dt.int32
+U32 = mybir.dt.uint32
+U8 = mybir.dt.uint8
+FP8X4 = mybir.dt.float8_e4m3fn_x4
+MULT = mybir.AluOpType.mult
+ADD = mybir.AluOpType.add
+
+P = 128
+PACK = 4
+K_PASS = P * PACK
+SEQ = 512
+HID = 2048
+HEAD = 128
+HALF = HEAD // 2
+K_GROUPS = HID // K_PASS
+ROW_SETS = SEQ // P
+N_TILE = 512
+HEADS_PER_TILE = N_TILE // HEAD
+LOAD_COLS = 1024
+WORDS_PER_PASS = K_PASS // 2
+QUADRANTS = 4
+LIVE_ROWS = 4
+
+FLOPS = 2 * SEQ * HID * (2048 + 1024 + 1024)
+
+
+def tile_selfmha_pa_kernel(
+    tc, x, Wq_words, Wq_scales, Wk_words, Wk_scales, Wv_words, Wv_scales, cos, sin, out_0, out_1, out_2
+):
+    nc = tc.nc
+    weights = [
+        ("q", Wq_words, Wq_scales, out_0, 2048, True),
+        ("k", Wk_words, Wk_scales, out_1, 1024, True),
+        ("v", Wv_words, Wv_scales, out_2, 1024, False),
+    ]
+
+    with ExitStack() as ctx:
+        keep = ctx.enter_context(tc.tile_pool(name="keep", bufs=1))
+        stage = ctx.enter_context(tc.tile_pool(name="stage", bufs=2))
+        results = ctx.enter_context(tc.tile_pool(name="results", bufs=8))
+        psum = ctx.enter_context(tc.psum_pool(name="psum", bufs=8))
+
+        ident = keep.tile([P, P], F32)
+        make_identity(nc, ident[:])
+
+        planes = {}
+        for name, words, scales, out, n_cols, rope in weights:
+            planes[name] = keep.tile([P, n_cols], U8, name="planes_%s" % name, align_bytes=64)
+            nc.vector.memset(planes[name][:].bitcast(I32), 0)
+
+        def load_planes(name, scales):
+            for quadrant in range(QUADRANTS):
+                nc.sync.dma_start(
+                    out=planes[name][32 * quadrant : 32 * quadrant + K_GROUPS * LIVE_ROWS, :].bitcast(I32),
+                    in_=scales[:, LIVE_ROWS * quadrant : LIVE_ROWS * (quadrant + 1), :].bitcast(I32),
+                )
+
+        w_tiles = {}
+
+        def load_words(name, words, block):
+            for g in range(K_GROUPS):
+                w_tile = keep.tile([P, LOAD_COLS], U32, name="w_%s%d_%d" % (name, block, g), align_bytes=64)
+                row = words[g].rearrange("p n t -> p (n t)")
+                nc.sync.dma_start(
+                    out=w_tile[:].bitcast(I32),
+                    in_=row[:, PACK * LOAD_COLS * block : PACK * LOAD_COLS * (block + 1)].bitcast(I32),
+                )
+                w_tiles[(name, block, g)] = w_tile
+
+        x_rows = x[0].rearrange("(p r) k -> p r k", r=ROW_SETS)
+        x_sets = []
+        for r in range(ROW_SETS):
+            x_set = keep.tile([P, HID], BF16, name="x_set%d" % r)
+            nc.sync.dma_start(out=x_set[:], in_=x_rows[:, r, :])
+            x_sets.append(x_set)
+
+        load_planes("q", Wq_scales)
+        load_words("q", Wq_words, 0)
+        cos_bf = keep.tile([P, ROW_SETS, HEAD], BF16)
+        sin_bf = keep.tile([P, ROW_SETS, HEAD], BF16)
+        nc.sync.dma_start(out=cos_bf[:], in_=cos.rearrange("(p r) d -> p r d", r=ROW_SETS))
+        nc.sync.dma_start(out=sin_bf[:], in_=sin.rearrange("(p r) d -> p r d", r=ROW_SETS))
+        load_planes("k", Wk_scales)
+        load_planes("v", Wv_scales)
+        load_words("q", Wq_words, 1)
+        load_words("k", Wk_words, 0)
+        load_words("v", Wv_words, 0)
+
+        x_codes = keep.tile([P, ROW_SETS, K_GROUPS * P], U32, align_bytes=64)
+        x_scales = keep.tile([P, ROW_SETS, K_GROUPS * P], U8, align_bytes=64)
+        for r in range(ROW_SETS):
+            x_words = x_sets[r][:].bitcast(F32)
+            grouped = stage.tile([P, K_GROUPS * P * PACK], BF16, align_bytes=64)
+            grouped_words = grouped[:].bitcast(F32).rearrange("p (g s u) -> p g s u", g=K_GROUPS, u=2)
+            for pair in range(K_GROUPS // 2):
+                bank = psum.tile([P, N_TILE], F32, tag="bank")
+                flipped = bank[:].rearrange("p (g u s) -> p g u s", g=2, u=2)
+                for i in range(2):
+                    g = 2 * pair + i
+                    for u in range(2):
+                        nc.tensor.transpose(
+                            flipped[:, i, u, :],
+                            x_words[:, WORDS_PER_PASS * g + u : WORDS_PER_PASS * (g + 1) : 2],
+                            ident[:],
+                        )
+                side_by_side = flipped.rearrange("p g u s -> p g s u")
+                if pair == 0:
+                    nc.vector.tensor_copy(out=grouped_words[:, 0:2], in_=side_by_side)
+                else:
+                    nc.scalar.copy(out=grouped_words[:, 2:4], in_=side_by_side)
+            nc.vector.quantize_mx(
+                out=x_codes[:, r, :].bitcast(FP8X4), scales=x_scales[:, r, :], in_=grouped[:]
+            )
+
+        cos_f = keep.tile([P, ROW_SETS, HEAD], F32)
+        sin_crossed = keep.tile([P, ROW_SETS, HEAD], F32)
+        nc.vector.tensor_copy(out=cos_f[:], in_=cos_bf[:])
+        nc.vector.tensor_copy(out=sin_crossed[:, :, 0:HALF], in_=sin_bf[:, :, HALF:HEAD])
+        nc.vector.tensor_scalar_mul(out=sin_crossed[:, :, HALF:HEAD], in0=sin_bf[:, :, 0:HALF], scalar1=-1.0)
+
+        first_group = True
+        for name, words, scales, out, n_cols, rope in weights:
+            for c0 in range(0, n_cols, N_TILE):
+                block = c0 // LOAD_COLS
+                in_block = c0 % LOAD_COLS
+                accs = []
+                for r in range(ROW_SETS):
+                    acc = psum.tile([P, N_TILE], F32, tag="bank")
+                    accs.append(acc)
+                if first_group:
+                    order = [(r, g) for g in range(K_GROUPS) for r in range(ROW_SETS)]
+                else:
+                    order = [(r, g) for r in range(ROW_SETS) for g in range(K_GROUPS)]
+                first_group = False
+                for r, g in order:
+                    nc.tensor.matmul_mx(
+                        out=accs[r][:],
+                        lhsT=x_codes[:, r, P * g : P * (g + 1)].bitcast(FP8X4),
+                        lhsT_scale=x_scales[:, r, P * g : P * (g + 1)],
+                        rhs=w_tiles[(name, block, g)][:, in_block : in_block + N_TILE].bitcast(FP8X4),
+                        rhs_scale=planes[name][LIVE_ROWS * g : P, c0 : c0 + N_TILE],
+                        start=(g == 0),
+                        stop=(g == K_GROUPS - 1),
+                    )
+
+                result = results.tile([P, HEADS_PER_TILE, ROW_SETS, HEAD], F32)
+                if rope:
+                    crossed = stage.tile([P, HEADS_PER_TILE, ROW_SETS, HEAD], F32)
+                    for r in range(ROW_SETS):
+                        by_head = accs[r][:].rearrange("p (h d) -> p h d", d=HEAD)
+                        shape = [P, HEADS_PER_TILE, HEAD]
+                        nc.vector.tensor_tensor(
+                            out=result[:, :, r, :], in0=by_head,
+                            in1=cos_f[:, r, :].unsqueeze(1).to_broadcast(shape), op=MULT,
+                        )
+                        nc.vector.tensor_tensor(
+                            out=crossed[:, :, r, :], in0=by_head,
+                            in1=sin_crossed[:, r, :].unsqueeze(1).to_broadcast(shape), op=MULT,
+                        )
+                    straight_rows = result[:].rearrange("p h r d -> p (h r) d")
+                    crossed_rows = crossed[:].rearrange("p h r d -> p (h r) d")
+                    nc.gpsimd.tensor_tensor(
+                        out=straight_rows[:, :, 0:HALF], in0=straight_rows[:, :, 0:HALF],
+                        in1=crossed_rows[:, :, HALF:HEAD], op=ADD,
+                    )
+                    nc.gpsimd.tensor_tensor(
+                        out=straight_rows[:, :, HALF:HEAD], in0=straight_rows[:, :, HALF:HEAD],
+                        in1=crossed_rows[:, :, 0:HALF], op=ADD,
+                    )
+                else:
+                    for r in range(ROW_SETS):
+                        nc.scalar.copy(
+                            out=result[:, :, r, :], in_=accs[r][:].rearrange("p (h d) -> p h d", d=HEAD)
+                        )
+                h0 = c0 // HEAD
+                nc.sync.dma_start(
+                    out=out[0, h0 : h0 + HEADS_PER_TILE].rearrange("h (p r) d -> p h (r d)", r=ROW_SETS),
+                    in_=result[:].rearrange("p h r d -> p h (r d)"),
+                )

@@ -19,16 +19,18 @@ SEQ = 512
 HID = 2048
 HEAD = 128
 HALF = HEAD // 2
+Q_COLS, K_COLS, V_COLS = 2048, 1024, 1024
 K_GROUPS = HID // K_PASS
 ROW_SETS = SEQ // P
 N_TILE = 512
 HEADS_PER_TILE = N_TILE // HEAD
-LOAD_COLS = 1024
 WORDS_PER_PASS = K_PASS // 2
 QUADRANTS = 4
 LIVE_ROWS = 4
+ROPE_GROUPS = (Q_COLS + K_COLS) // N_TILE
+PLAIN_BANKS = (V_COLS // N_TILE) * ROW_SETS
 
-FLOPS = 2 * SEQ * HID * (2048 + 1024 + 1024)
+FLOPS = 2 * SEQ * HID * (Q_COLS + K_COLS + V_COLS)
 
 
 def tile_selfmha_pa_kernel(
@@ -36,15 +38,16 @@ def tile_selfmha_pa_kernel(
 ):
     nc = tc.nc
     weights = [
-        ("q", Wq_words, Wq_scales, out_0, 2048, True),
-        ("k", Wk_words, Wk_scales, out_1, 1024, True),
-        ("v", Wv_words, Wv_scales, out_2, 1024, False),
+        ("q", Wq_words, Wq_scales, out_0, Q_COLS, True),
+        ("k", Wk_words, Wk_scales, out_1, K_COLS, True),
+        ("v", Wv_words, Wv_scales, out_2, V_COLS, False),
     ]
 
     with ExitStack() as ctx:
         keep = ctx.enter_context(tc.tile_pool(name="keep", bufs=1))
         stage = ctx.enter_context(tc.tile_pool(name="stage", bufs=2))
-        results = ctx.enter_context(tc.tile_pool(name="results", bufs=8))
+        roped = ctx.enter_context(tc.tile_pool(name="roped", bufs=ROPE_GROUPS))
+        plain = ctx.enter_context(tc.tile_pool(name="plain", bufs=PLAIN_BANKS))
         psum = ctx.enter_context(tc.psum_pool(name="psum", bufs=8))
 
         ident = keep.tile([P, P], F32)
@@ -64,15 +67,14 @@ def tile_selfmha_pa_kernel(
 
         w_tiles = {}
 
-        def load_words(name, words, block):
+        def load_words(name, words, c0):
             for g in range(K_GROUPS):
-                w_tile = keep.tile([P, LOAD_COLS], U32, name="w_%s%d_%d" % (name, block, g), align_bytes=64)
+                w_tile = keep.tile([P, N_TILE], U32, name="w_%s%d_%d" % (name, c0, g), align_bytes=64)
                 row = words[g].rearrange("p n t -> p (n t)")
                 nc.sync.dma_start(
-                    out=w_tile[:].bitcast(I32),
-                    in_=row[:, PACK * LOAD_COLS * block : PACK * LOAD_COLS * (block + 1)].bitcast(I32),
+                    out=w_tile[:].bitcast(I32), in_=row[:, PACK * c0 : PACK * (c0 + N_TILE)].bitcast(I32)
                 )
-                w_tiles[(name, block, g)] = w_tile
+                w_tiles[(name, c0, g)] = w_tile
 
         x_rows = x[0].rearrange("(p r) k -> p r k", r=ROW_SETS)
         x_sets = []
@@ -87,11 +89,14 @@ def tile_selfmha_pa_kernel(
         sin_bf = keep.tile([P, ROW_SETS, HEAD], BF16)
         nc.sync.dma_start(out=cos_bf[:], in_=cos.rearrange("(p r) d -> p r d", r=ROW_SETS))
         nc.sync.dma_start(out=sin_bf[:], in_=sin.rearrange("(p r) d -> p r d", r=ROW_SETS))
+        for c0 in range(N_TILE, Q_COLS, N_TILE):
+            load_words("q", Wq_words, c0)
         load_planes("k", Wk_scales)
         load_planes("v", Wv_scales)
-        load_words("q", Wq_words, 1)
-        load_words("k", Wk_words, 0)
-        load_words("v", Wv_words, 0)
+        for c0 in range(0, K_COLS, N_TILE):
+            load_words("k", Wk_words, c0)
+        for c0 in range(0, V_COLS, N_TILE):
+            load_words("v", Wv_words, c0)
 
         x_codes = keep.tile([P, ROW_SETS, K_GROUPS * P], U32, align_bytes=64)
         x_scales = keep.tile([P, ROW_SETS, K_GROUPS * P], U8, align_bytes=64)
@@ -119,68 +124,60 @@ def tile_selfmha_pa_kernel(
                 out=x_codes[:, r, :].bitcast(FP8X4), scales=x_scales[:, r, :], in_=grouped[:]
             )
 
-        cos_f = keep.tile([P, ROW_SETS, HEAD], F32)
-        sin_crossed = keep.tile([P, ROW_SETS, HEAD], F32)
-        nc.vector.tensor_copy(out=cos_f[:], in_=cos_bf[:])
-        nc.vector.tensor_copy(out=sin_crossed[:, :, 0:HALF], in_=sin_bf[:, :, HALF:HEAD])
-        nc.vector.tensor_scalar_mul(out=sin_crossed[:, :, HALF:HEAD], in0=sin_bf[:, :, 0:HALF], scalar1=-1.0)
+        factors = keep.tile([P, ROW_SETS, 2, HEAD], F32)
+        nc.vector.tensor_copy(out=factors[:, :, 0, :], in_=cos_bf[:])
+        nc.vector.tensor_copy(out=factors[:, :, 1, 0:HALF], in_=sin_bf[:, :, HALF:HEAD])
+        nc.vector.tensor_scalar_mul(out=factors[:, :, 1, HALF:HEAD], in0=sin_bf[:, :, 0:HALF], scalar1=-1.0)
 
-        first_group = True
         for name, words, scales, out, n_cols, rope in weights:
             for c0 in range(0, n_cols, N_TILE):
-                block = c0 // LOAD_COLS
-                in_block = c0 % LOAD_COLS
                 accs = []
-                for r in range(ROW_SETS):
-                    acc = psum.tile([P, N_TILE], F32, tag="bank")
-                    accs.append(acc)
-                if first_group:
-                    order = [(r, g) for g in range(K_GROUPS) for r in range(ROW_SETS)]
-                else:
-                    order = [(r, g) for r in range(ROW_SETS) for g in range(K_GROUPS)]
-                first_group = False
-                for r, g in order:
-                    nc.tensor.matmul_mx(
-                        out=accs[r][:],
-                        lhsT=x_codes[:, r, P * g : P * (g + 1)].bitcast(FP8X4),
-                        lhsT_scale=x_scales[:, r, P * g : P * (g + 1)],
-                        rhs=w_tiles[(name, block, g)][:, in_block : in_block + N_TILE].bitcast(FP8X4),
-                        rhs_scale=planes[name][LIVE_ROWS * g : P, c0 : c0 + N_TILE],
-                        start=(g == 0),
-                        stop=(g == K_GROUPS - 1),
-                    )
+                for r0 in range(0, ROW_SETS, 2):
+                    for r in (r0, r0 + 1):
+                        acc = psum.tile([P, N_TILE], F32, tag="bank")
+                        accs.append(acc)
+                    for g in range(K_GROUPS):
+                        for r in (r0, r0 + 1):
+                            nc.tensor.matmul_mx(
+                                out=accs[r][:],
+                                lhsT=x_codes[:, r, P * g : P * (g + 1)].bitcast(FP8X4),
+                                lhsT_scale=x_scales[:, r, P * g : P * (g + 1)],
+                                rhs=w_tiles[(name, c0, g)][:].bitcast(FP8X4),
+                                rhs_scale=planes[name][LIVE_ROWS * g : P, c0 : c0 + N_TILE],
+                                start=(g == 0),
+                                stop=(g == K_GROUPS - 1),
+                            )
 
-                result = results.tile([P, HEADS_PER_TILE, ROW_SETS, HEAD], F32)
-                if rope:
-                    crossed = stage.tile([P, HEADS_PER_TILE, ROW_SETS, HEAD], F32)
-                    for r in range(ROW_SETS):
-                        by_head = accs[r][:].rearrange("p (h d) -> p h d", d=HEAD)
-                        shape = [P, HEADS_PER_TILE, HEAD]
-                        nc.vector.tensor_tensor(
-                            out=result[:, :, r, :], in0=by_head,
-                            in1=cos_f[:, r, :].unsqueeze(1).to_broadcast(shape), op=MULT,
-                        )
-                        nc.vector.tensor_tensor(
-                            out=crossed[:, :, r, :], in0=by_head,
-                            in1=sin_crossed[:, r, :].unsqueeze(1).to_broadcast(shape), op=MULT,
-                        )
-                    straight_rows = result[:].rearrange("p h r d -> p (h r) d")
-                    crossed_rows = crossed[:].rearrange("p h r d -> p (h r) d")
-                    nc.gpsimd.tensor_tensor(
-                        out=straight_rows[:, :, 0:HALF], in0=straight_rows[:, :, 0:HALF],
-                        in1=crossed_rows[:, :, HALF:HEAD], op=ADD,
-                    )
-                    nc.gpsimd.tensor_tensor(
-                        out=straight_rows[:, :, HALF:HEAD], in0=straight_rows[:, :, HALF:HEAD],
-                        in1=crossed_rows[:, :, 0:HALF], op=ADD,
-                    )
-                else:
-                    for r in range(ROW_SETS):
-                        nc.scalar.copy(
-                            out=result[:, :, r, :], in_=accs[r][:].rearrange("p (h d) -> p h d", d=HEAD)
-                        )
                 h0 = c0 // HEAD
+                out_rows = out[0, h0 : h0 + HEADS_PER_TILE].rearrange("h (p r) d -> p h r d", r=ROW_SETS)
+                if not rope:
+                    for r in range(ROW_SETS):
+                        copied = plain.tile([P, HEADS_PER_TILE, HEAD], F32)
+                        nc.scalar.copy(out=copied[:], in_=accs[r][:].rearrange("p (h d) -> p h d", d=HEAD))
+                        nc.scalar.dma_start(out=out_rows[:, :, r, :], in_=copied[:])
+                    continue
+
+                products = roped.tile([P, 2, HEADS_PER_TILE, ROW_SETS, HEAD], F32)
+                both = [P, 2, HEADS_PER_TILE, HEAD]
+                for r in range(ROW_SETS):
+                    by_head = accs[r][:].rearrange("p (h d) -> p h d", d=HEAD)
+                    nc.vector.tensor_tensor(
+                        out=products[:, :, :, r, :],
+                        in0=by_head.unsqueeze(1).to_broadcast(both),
+                        in1=factors[:, r].unsqueeze(2).to_broadcast(both),
+                        op=MULT,
+                    )
+                last_rope_group = name == "k" and c0 == K_COLS - N_TILE
+                adder = nc.vector if last_rope_group else nc.gpsimd
+                straight = products[:, 0].rearrange("p h r d -> p (h r) d")
+                crossed = products[:, 1].rearrange("p h r d -> p (h r) d")
+                adder.tensor_tensor(
+                    out=straight[:, :, 0:HALF], in0=straight[:, :, 0:HALF], in1=crossed[:, :, HALF:HEAD], op=ADD
+                )
+                adder.tensor_tensor(
+                    out=straight[:, :, HALF:HEAD], in0=straight[:, :, HALF:HEAD], in1=crossed[:, :, 0:HALF], op=ADD
+                )
                 nc.sync.dma_start(
-                    out=out[0, h0 : h0 + HEADS_PER_TILE].rearrange("h (p r) d -> p h (r d)", r=ROW_SETS),
-                    in_=result[:].rearrange("p h r d -> p h (r d)"),
+                    out=out_rows.rearrange("p h r d -> p h (r d)"),
+                    in_=products[:, 0].rearrange("p h r d -> p h (r d)"),
                 )

@@ -28,7 +28,7 @@ WORDS_PER_PASS = K_PASS // 2
 QUADRANTS = 4
 LIVE_ROWS = 4
 ROPE_GROUPS = (Q_COLS + K_COLS) // N_TILE
-PLAIN_BANKS = (V_COLS // N_TILE) * ROW_SETS
+PLAIN_GROUPS = V_COLS // N_TILE
 
 FLOPS = 2 * SEQ * HID * (Q_COLS + K_COLS + V_COLS)
 
@@ -47,7 +47,7 @@ def tile_selfmha_pa_kernel(
         keep = ctx.enter_context(tc.tile_pool(name="keep", bufs=1))
         stage = ctx.enter_context(tc.tile_pool(name="stage", bufs=2))
         roped = ctx.enter_context(tc.tile_pool(name="roped", bufs=ROPE_GROUPS))
-        plain = ctx.enter_context(tc.tile_pool(name="plain", bufs=PLAIN_BANKS))
+        plain = ctx.enter_context(tc.tile_pool(name="plain", bufs=PLAIN_GROUPS))
         psum = ctx.enter_context(tc.psum_pool(name="psum", bufs=8))
 
         ident = keep.tile([P, P], F32)
@@ -65,16 +65,17 @@ def tile_selfmha_pa_kernel(
                     in_=scales[:, LIVE_ROWS * quadrant : LIVE_ROWS * (quadrant + 1), :].bitcast(I32),
                 )
 
-        w_tiles = {}
+        w_words = {}
 
-        def load_words(name, words, c0):
+        def load_words(name, words, c0, n_cols):
             for g in range(K_GROUPS):
-                w_tile = keep.tile([P, N_TILE], U32, name="w_%s%d_%d" % (name, c0, g), align_bytes=64)
+                w_tile = keep.tile([P, n_cols], U32, name="w_%s%d_%d" % (name, c0, g), align_bytes=64)
                 row = words[g].rearrange("p n t -> p (n t)")
                 nc.sync.dma_start(
-                    out=w_tile[:].bitcast(I32), in_=row[:, PACK * c0 : PACK * (c0 + N_TILE)].bitcast(I32)
+                    out=w_tile[:].bitcast(I32), in_=row[:, PACK * c0 : PACK * (c0 + n_cols)].bitcast(I32)
                 )
-                w_tiles[(name, c0, g)] = w_tile
+                for c in range(0, n_cols, N_TILE):
+                    w_words[(name, c0 + c, g)] = w_tile[:, c : c + N_TILE]
 
         x_rows = x[0].rearrange("(p r) k -> p r k", r=ROW_SETS)
         x_sets = []
@@ -84,19 +85,17 @@ def tile_selfmha_pa_kernel(
             x_sets.append(x_set)
 
         load_planes("q", Wq_scales)
-        load_words("q", Wq_words, 0)
+        load_words("q", Wq_words, 0, N_TILE)
         cos_bf = keep.tile([P, ROW_SETS, HEAD], BF16)
         sin_bf = keep.tile([P, ROW_SETS, HEAD], BF16)
         nc.sync.dma_start(out=cos_bf[:], in_=cos.rearrange("(p r) d -> p r d", r=ROW_SETS))
         nc.sync.dma_start(out=sin_bf[:], in_=sin.rearrange("(p r) d -> p r d", r=ROW_SETS))
-        for c0 in range(N_TILE, Q_COLS, N_TILE):
-            load_words("q", Wq_words, c0)
+        load_words("q", Wq_words, N_TILE, N_TILE)
+        load_words("q", Wq_words, 2 * N_TILE, 2 * N_TILE)
         load_planes("k", Wk_scales)
         load_planes("v", Wv_scales)
-        for c0 in range(0, K_COLS, N_TILE):
-            load_words("k", Wk_words, c0)
-        for c0 in range(0, V_COLS, N_TILE):
-            load_words("v", Wv_words, c0)
+        load_words("k", Wk_words, 0, 2 * N_TILE)
+        load_words("v", Wv_words, 0, 2 * N_TILE)
 
         x_codes = keep.tile([P, ROW_SETS, K_GROUPS * P], U32, align_bytes=64)
         x_scales = keep.tile([P, ROW_SETS, K_GROUPS * P], U8, align_bytes=64)
@@ -142,19 +141,21 @@ def tile_selfmha_pa_kernel(
                                 out=accs[r][:],
                                 lhsT=x_codes[:, r, P * g : P * (g + 1)].bitcast(FP8X4),
                                 lhsT_scale=x_scales[:, r, P * g : P * (g + 1)],
-                                rhs=w_tiles[(name, c0, g)][:].bitcast(FP8X4),
+                                rhs=w_words[(name, c0, g)].bitcast(FP8X4),
                                 rhs_scale=planes[name][LIVE_ROWS * g : P, c0 : c0 + N_TILE],
                                 start=(g == 0),
                                 stop=(g == K_GROUPS - 1),
                             )
 
                 h0 = c0 // HEAD
-                out_rows = out[0, h0 : h0 + HEADS_PER_TILE].rearrange("h (p r) d -> p h r d", r=ROW_SETS)
+                out_rows = out[0, h0 : h0 + HEADS_PER_TILE].rearrange("h (p r) d -> p h (r d)", r=ROW_SETS)
                 if not rope:
+                    copied = plain.tile([P, HEADS_PER_TILE, ROW_SETS, HEAD], F32)
                     for r in range(ROW_SETS):
-                        copied = plain.tile([P, HEADS_PER_TILE, HEAD], F32)
-                        nc.scalar.copy(out=copied[:], in_=accs[r][:].rearrange("p (h d) -> p h d", d=HEAD))
-                        nc.scalar.dma_start(out=out_rows[:, :, r, :], in_=copied[:])
+                        nc.scalar.copy(
+                            out=copied[:, :, r, :], in_=accs[r][:].rearrange("p (h d) -> p h d", d=HEAD)
+                        )
+                    nc.scalar.dma_start(out=out_rows, in_=copied[:].rearrange("p h r d -> p h (r d)"))
                     continue
 
                 products = roped.tile([P, 2, HEADS_PER_TILE, ROW_SETS, HEAD], F32)
@@ -177,7 +178,4 @@ def tile_selfmha_pa_kernel(
                 adder.tensor_tensor(
                     out=straight[:, :, HALF:HEAD], in0=straight[:, :, HALF:HEAD], in1=crossed[:, :, 0:HALF], op=ADD
                 )
-                nc.sync.dma_start(
-                    out=out_rows.rearrange("p h r d -> p h (r d)"),
-                    in_=products[:, 0].rearrange("p h r d -> p h (r d)"),
-                )
+                nc.sync.dma_start(out=out_rows, in_=products[:, 0].rearrange("p h r d -> p h (r d)"))

@@ -130,13 +130,14 @@ def tile_selfmha_pa_kernel(
 
         for name, words, scales, out, n_cols, rope in weights:
             for c0 in range(0, n_cols, N_TILE):
+                together = 2 if name == "q" and c0 == 0 else 1
                 accs = []
-                for r0 in range(0, ROW_SETS, 2):
-                    for r in (r0, r0 + 1):
+                for r0 in range(0, ROW_SETS, together):
+                    for r in range(r0, r0 + together):
                         acc = psum.tile([P, N_TILE], F32, tag="bank")
                         accs.append(acc)
                     for g in range(K_GROUPS):
-                        for r in (r0, r0 + 1):
+                        for r in range(r0, r0 + together):
                             nc.tensor.matmul_mx(
                                 out=accs[r][:],
                                 lhsT=x_codes[:, r, P * g : P * (g + 1)].bitcast(FP8X4),
@@ -169,13 +170,14 @@ def tile_selfmha_pa_kernel(
                         op=MULT,
                     )
                 last_rope_group = name == "k" and c0 == K_COLS - N_TILE
-                adder = nc.vector if last_rope_group else nc.gpsimd
+                first_adder = nc.vector if last_rope_group else nc.gpsimd
+                second_adder = nc.vector if name == "k" else nc.gpsimd
                 straight = products[:, 0].rearrange("p h r d -> p (h r) d")
                 crossed = products[:, 1].rearrange("p h r d -> p (h r) d")
-                adder.tensor_tensor(
+                first_adder.tensor_tensor(
                     out=straight[:, :, 0:HALF], in0=straight[:, :, 0:HALF], in1=crossed[:, :, HALF:HEAD], op=ADD
                 )
-                adder.tensor_tensor(
+                second_adder.tensor_tensor(
                     out=straight[:, :, HALF:HEAD], in0=straight[:, :, HALF:HEAD], in1=crossed[:, :, 0:HALF], op=ADD
                 )
                 nc.sync.dma_start(out=out_rows, in_=products[:, 0].rearrange("p h r d -> p h (r d)"))

@@ -128,6 +128,7 @@ def tile_selfmha_pa_kernel(
         nc.vector.tensor_copy(out=factors[:, :, 1, 0:HALF], in_=sin_bf[:, :, HALF:HEAD])
         nc.vector.tensor_scalar_mul(out=factors[:, :, 1, HALF:HEAD], in0=sin_bf[:, :, 0:HALF], scalar1=-1.0)
 
+        waiting = []
         for name, words, scales, out, n_cols, rope in weights:
             for c0 in range(0, n_cols, N_TILE):
                 together = 2 if name == "q" and c0 == 0 else 1
@@ -177,7 +178,15 @@ def tile_selfmha_pa_kernel(
                 first_adder.tensor_tensor(
                     out=straight[:, :, 0:HALF], in0=straight[:, :, 0:HALF], in1=crossed[:, :, HALF:HEAD], op=ADD
                 )
-                second_adder.tensor_tensor(
-                    out=straight[:, :, HALF:HEAD], in0=straight[:, :, HALF:HEAD], in1=crossed[:, :, 0:HALF], op=ADD
-                )
-                nc.sync.dma_start(out=out_rows, in_=products[:, 0].rearrange("p h r d -> p h (r d)"))
+                waiting.append((second_adder, straight, crossed, out_rows, products))
+                if name == "k" and not last_rope_group:
+                    continue
+                for adder, straight, crossed, out_rows, products in waiting:
+                    adder.tensor_tensor(
+                        out=straight[:, :, HALF:HEAD],
+                        in0=straight[:, :, HALF:HEAD],
+                        in1=crossed[:, :, 0:HALF],
+                        op=ADD,
+                    )
+                    nc.sync.dma_start(out=out_rows, in_=products[:, 0].rearrange("p h r d -> p h (r d)"))
+                waiting.clear()

@@ -47,7 +47,7 @@ def tile_selfmha_pa_kernel(
         keep = ctx.enter_context(tc.tile_pool(name="keep", bufs=1))
         stage = ctx.enter_context(tc.tile_pool(name="stage", bufs=2))
         roped = ctx.enter_context(tc.tile_pool(name="roped", bufs=ROPE_GROUPS))
-        plain = ctx.enter_context(tc.tile_pool(name="plain", bufs=PLAIN_GROUPS))
+        plain = ctx.enter_context(tc.tile_pool(name="plain", bufs=PLAIN_GROUPS + 1))
         psum = ctx.enter_context(tc.psum_pool(name="psum", bufs=8))
 
         ident = keep.tile([P, P], F32)
@@ -130,29 +130,34 @@ def tile_selfmha_pa_kernel(
 
         waiting = []
         for name, words, scales, out, n_cols, rope in weights:
-            for c0 in range(0, n_cols, N_TILE):
+            groups = [(c0, N_TILE) for c0 in range(0, n_cols, N_TILE)]
+            if name == "v":
+                last_c0 = groups.pop()[0]
+                groups.extend([(last_c0, N_TILE // 2), (last_c0 + N_TILE // 2, N_TILE // 2)])
+            for c0, width in groups:
                 together = 2 if name == "q" and c0 == 0 else 1
                 accs = []
                 for r0 in range(0, ROW_SETS, together):
                     for r in range(r0, r0 + together):
-                        acc = psum.tile([P, N_TILE], F32, tag="bank")
+                        acc = psum.tile([P, width], F32, tag="bank")
                         accs.append(acc)
+                    tile_c0 = c0 - c0 % N_TILE
                     for g in range(K_GROUPS):
                         for r in range(r0, r0 + together):
                             nc.tensor.matmul_mx(
                                 out=accs[r][:],
                                 lhsT=x_codes[:, r, P * g : P * (g + 1)].bitcast(FP8X4),
                                 lhsT_scale=x_scales[:, r, P * g : P * (g + 1)],
-                                rhs=w_words[(name, c0, g)].bitcast(FP8X4),
-                                rhs_scale=planes[name][LIVE_ROWS * g : P, c0 : c0 + N_TILE],
+                                rhs=w_words[(name, tile_c0, g)][:, c0 - tile_c0 : c0 - tile_c0 + width].bitcast(FP8X4),
+                                rhs_scale=planes[name][LIVE_ROWS * g : P, c0 : c0 + width],
                                 start=(g == 0),
                                 stop=(g == K_GROUPS - 1),
                             )
 
                 h0 = c0 // HEAD
-                out_rows = out[0, h0 : h0 + HEADS_PER_TILE].rearrange("h (p r) d -> p h (r d)", r=ROW_SETS)
+                out_rows = out[0, h0 : h0 + width // HEAD].rearrange("h (p r) d -> p h (r d)", r=ROW_SETS)
                 if not rope:
-                    copied = plain.tile([P, HEADS_PER_TILE, ROW_SETS, HEAD], F32)
+                    copied = plain.tile([P, width // HEAD, ROW_SETS, HEAD], F32)
                     for r in range(ROW_SETS):
                         nc.scalar.copy(
                             out=copied[:, :, r, :], in_=accs[r][:].rearrange("p (h d) -> p h d", d=HEAD)

@@ -58,11 +58,11 @@ def tile_selfmha_pa_kernel(
             planes[name] = keep.tile([P, n_cols], U8, name="planes_%s" % name, align_bytes=64)
             nc.vector.memset(planes[name][:].bitcast(I32), 0)
 
-        def load_planes(name, scales):
+        def load_planes(name, scales, c0, c1):
             for quadrant in range(QUADRANTS):
                 nc.sync.dma_start(
-                    out=planes[name][32 * quadrant : 32 * quadrant + K_GROUPS * LIVE_ROWS, :].bitcast(I32),
-                    in_=scales[:, LIVE_ROWS * quadrant : LIVE_ROWS * (quadrant + 1), :].bitcast(I32),
+                    out=planes[name][32 * quadrant : 32 * quadrant + K_GROUPS * LIVE_ROWS, c0:c1].bitcast(I32),
+                    in_=scales[:, LIVE_ROWS * quadrant : LIVE_ROWS * (quadrant + 1), c0:c1].bitcast(I32),
                 )
 
         w_words = {}
@@ -84,16 +84,17 @@ def tile_selfmha_pa_kernel(
             nc.sync.dma_start(out=x_set[:], in_=x_rows[:, r, :])
             x_sets.append(x_set)
 
-        load_planes("q", Wq_scales)
+        load_planes("q", Wq_scales, 0, N_TILE)
         load_words("q", Wq_words, 0, N_TILE)
         cos_bf = keep.tile([P, ROW_SETS, HEAD], BF16)
         sin_bf = keep.tile([P, ROW_SETS, HEAD], BF16)
         nc.sync.dma_start(out=cos_bf[:], in_=cos.rearrange("(p r) d -> p r d", r=ROW_SETS))
         nc.sync.dma_start(out=sin_bf[:], in_=sin.rearrange("(p r) d -> p r d", r=ROW_SETS))
+        load_planes("q", Wq_scales, N_TILE, Q_COLS)
         load_words("q", Wq_words, N_TILE, N_TILE)
         load_words("q", Wq_words, 2 * N_TILE, 2 * N_TILE)
-        load_planes("k", Wk_scales)
-        load_planes("v", Wv_scales)
+        load_planes("k", Wk_scales, 0, K_COLS)
+        load_planes("v", Wv_scales, 0, V_COLS)
         load_words("k", Wk_words, 0, 2 * N_TILE)
         load_words("v", Wv_words, 0, 2 * N_TILE)
 

@@ -11,6 +11,7 @@ U8 = mybir.dt.uint8
 FP8X4 = mybir.dt.float8_e4m3fn_x4
 MULT = mybir.AluOpType.mult
 ADD = mybir.AluOpType.add
+SUBTRACT = mybir.AluOpType.subtract
 
 P = 128
 PACK = 4
@@ -86,10 +87,11 @@ def tile_selfmha_pa_kernel(
 
         load_planes("q", Wq_scales, 0, N_TILE)
         load_words("q", Wq_words, 0, N_TILE)
-        cos_bf = keep.tile([P, ROW_SETS, HEAD], BF16)
-        sin_bf = keep.tile([P, ROW_SETS, HEAD], BF16)
-        nc.sync.dma_start(out=cos_bf[:], in_=cos.rearrange("(p r) d -> p r d", r=ROW_SETS))
-        nc.sync.dma_start(out=sin_bf[:], in_=sin.rearrange("(p r) d -> p r d", r=ROW_SETS))
+        factors = keep.tile([P, ROW_SETS, 2, HEAD], BF16)
+        sin_rows = sin.rearrange("(p r) d -> p r d", r=ROW_SETS)
+        nc.sync.dma_start(out=factors[:, :, 0, :], in_=cos.rearrange("(p r) d -> p r d", r=ROW_SETS))
+        nc.sync.dma_start(out=factors[:, :, 1, 0:HALF], in_=sin_rows[:, :, HALF:HEAD])
+        nc.sync.dma_start(out=factors[:, :, 1, HALF:HEAD], in_=sin_rows[:, :, 0:HALF])
         load_planes("q", Wq_scales, N_TILE, Q_COLS)
         load_words("q", Wq_words, N_TILE, N_TILE)
         load_words("q", Wq_words, 2 * N_TILE, 2 * N_TILE)
@@ -124,12 +126,7 @@ def tile_selfmha_pa_kernel(
                 out=x_codes[:, r, :].bitcast(FP8X4), scales=x_scales[:, r, :], in_=grouped[:]
             )
 
-        factors = keep.tile([P, ROW_SETS, 2, HEAD], F32)
-        nc.vector.tensor_copy(out=factors[:, :, 0, :], in_=cos_bf[:])
-        nc.vector.tensor_copy(out=factors[:, :, 1, 0:HALF], in_=sin_bf[:, :, HALF:HEAD])
-        nc.vector.tensor_scalar_mul(out=factors[:, :, 1, HALF:HEAD], in0=sin_bf[:, :, 0:HALF], scalar1=-1.0)
 
-        waiting = []
         for name, words, scales, out, n_cols, rope in weights:
             groups = [(c0, N_TILE) for c0 in range(0, n_cols, N_TILE)]
             if name == "v":
@@ -178,21 +175,13 @@ def tile_selfmha_pa_kernel(
                     )
                 last_rope_group = name == "k" and c0 == K_COLS - N_TILE
                 first_adder = nc.vector if last_rope_group else nc.gpsimd
-                second_adder = nc.vector if name == "k" else nc.gpsimd
+                second_adder = first_adder
                 straight = products[:, 0].rearrange("p h r d -> p (h r) d")
                 crossed = products[:, 1].rearrange("p h r d -> p (h r) d")
                 first_adder.tensor_tensor(
-                    out=straight[:, :, 0:HALF], in0=straight[:, :, 0:HALF], in1=crossed[:, :, HALF:HEAD], op=ADD
+                    out=straight[:, :, 0:HALF], in0=straight[:, :, 0:HALF], in1=crossed[:, :, HALF:HEAD], op=SUBTRACT
                 )
-                waiting.append((second_adder, straight, crossed, out_rows, products))
-                if name == "k" and not last_rope_group:
-                    continue
-                for adder, straight, crossed, out_rows, products in waiting:
-                    adder.tensor_tensor(
-                        out=straight[:, :, HALF:HEAD],
-                        in0=straight[:, :, HALF:HEAD],
-                        in1=crossed[:, :, 0:HALF],
-                        op=ADD,
-                    )
-                    nc.sync.dma_start(out=out_rows, in_=products[:, 0].rearrange("p h r d -> p h (r d)"))
-                waiting.clear()
+                second_adder.tensor_tensor(
+                    out=straight[:, :, HALF:HEAD], in0=straight[:, :, HALF:HEAD], in1=crossed[:, :, 0:HALF], op=ADD
+                )
+                nc.sync.dma_start(out=out_rows, in_=products[:, 0].rearrange("p h r d -> p h (r d)"))

from contextlib import ExitStack

import concourse.mybir as mybir
from concourse.masks import make_identity

F32 = mybir.dt.float32
BF16 = mybir.dt.bfloat16
I32 = mybir.dt.int32
U32 = mybir.dt.uint32
U8 = mybir.dt.uint8
FP8X4 = mybir.dt.float8_e4m3fn_x4
MULT = mybir.AluOpType.mult
ADD = mybir.AluOpType.add
SUBTRACT = mybir.AluOpType.subtract

P = 128
PACK = 4
K_PASS = P * PACK
SEQ = 512
HID = 2048
HEAD = 128
HALF = HEAD // 2
Q_COLS, K_COLS, V_COLS = 2048, 1024, 1024
K_GROUPS = HID // K_PASS
ROW_SETS = SEQ // P
N_TILE = 512
HEADS_PER_TILE = N_TILE // HEAD
WORDS_PER_PASS = K_PASS // 2
QUADRANTS = 4
LIVE_ROWS = 4
ROPE_GROUPS = (Q_COLS + K_COLS) // N_TILE
PLAIN_GROUPS = V_COLS // N_TILE

FLOPS = 2 * SEQ * HID * (Q_COLS + K_COLS + V_COLS)


def tile_selfmha_pa_kernel(
    tc, x, Wq_words, Wq_scales, Wk_words, Wk_scales, Wv_words, Wv_scales, cos, sin, out_0, out_1, out_2
):
    nc = tc.nc
    weights = [
        ("q", Wq_words, Wq_scales, out_0, Q_COLS, True),
        ("k", Wk_words, Wk_scales, out_1, K_COLS, True),
        ("v", Wv_words, Wv_scales, out_2, V_COLS, False),
    ]

    with ExitStack() as ctx:
        keep = ctx.enter_context(tc.tile_pool(name="keep", bufs=1))
        stage = ctx.enter_context(tc.tile_pool(name="stage", bufs=2))
        roped = ctx.enter_context(tc.tile_pool(name="roped", bufs=ROPE_GROUPS))
        plain = ctx.enter_context(tc.tile_pool(name="plain", bufs=PLAIN_GROUPS + 1))
        psum = ctx.enter_context(tc.psum_pool(name="psum", bufs=8))

        ident = keep.tile([P, P], F32)
        make_identity(nc, ident[:])

        planes = {}
        for name, words, scales, out, n_cols, rope in weights:
            planes[name] = keep.tile([P, n_cols], U8, name="planes_%s" % name, align_bytes=64)
            nc.vector.memset(planes[name][:].bitcast(I32), 0)

        def load_planes(name, scales, c0, c1):
            for quadrant in range(QUADRANTS):
                nc.sync.dma_start(
                    out=planes[name][32 * quadrant : 32 * quadrant + K_GROUPS * LIVE_ROWS, c0:c1].bitcast(I32),
                    in_=scales[:, LIVE_ROWS * quadrant : LIVE_ROWS * (quadrant + 1), c0:c1].bitcast(I32),
                )

        w_words = {}

        def load_words(name, words, c0, n_cols):
            for g in range(K_GROUPS):
                w_tile = keep.tile([P, n_cols], U32, name="w_%s%d_%d" % (name, c0, g), align_bytes=64)
                row = words[g].rearrange("p n t -> p (n t)")
                nc.sync.dma_start(
                    out=w_tile[:].bitcast(I32), in_=row[:, PACK * c0 : PACK * (c0 + n_cols)].bitcast(I32)
                )
                for c in range(0, n_cols, N_TILE):
                    w_words[(name, c0 + c, g)] = w_tile[:, c : c + N_TILE]

        x_rows = x[0].rearrange("(p r) k -> p r k", r=ROW_SETS)
        x_sets = []
        for r in range(ROW_SETS):
            x_set = keep.tile([P, HID], BF16, name="x_set%d" % r)
            nc.sync.dma_start(out=x_set[:], in_=x_rows[:, r, :])
            x_sets.append(x_set)

        load_planes("q", Wq_scales, 0, N_TILE)
        load_words("q", Wq_words, 0, N_TILE)
        factors = keep.tile([P, ROW_SETS, 2, HEAD], BF16)
        sin_rows = sin.rearrange("(p r) d -> p r d", r=ROW_SETS)
        nc.sync.dma_start(out=factors[:, :, 0, :], in_=cos.rearrange("(p r) d -> p r d", r=ROW_SETS))
        nc.sync.dma_start(out=factors[:, :, 1, 0:HALF], in_=sin_rows[:, :, HALF:HEAD])
        nc.sync.dma_start(out=factors[:, :, 1, HALF:HEAD], in_=sin_rows[:, :, 0:HALF])
        load_planes("q", Wq_scales, N_TILE, Q_COLS)
        load_words("q", Wq_words, N_TILE, N_TILE)
        load_words("q", Wq_words, 2 * N_TILE, 2 * N_TILE)
        load_planes("k", Wk_scales, 0, K_COLS)
        load_planes("v", Wv_scales, 0, V_COLS)
        load_words("k", Wk_words, 0, 2 * N_TILE)
        load_words("v", Wv_words, 0, 2 * N_TILE)

        x_codes = keep.tile([P, ROW_SETS, K_GROUPS * P], U32, align_bytes=64)
        x_scales = keep.tile([P, ROW_SETS, K_GROUPS * P], U8, align_bytes=64)
        for r in range(ROW_SETS):
            x_words = x_sets[r][:].bitcast(F32)
            grouped = stage.tile([P, K_GROUPS * P * PACK], BF16, align_bytes=64)
            grouped_words = grouped[:].bitcast(F32).rearrange("p (g s u) -> p g s u", g=K_GROUPS, u=2)
            for pair in range(K_GROUPS // 2):
                bank = psum.tile([P, N_TILE], F32, tag="bank")
                flipped = bank[:].rearrange("p (g u s) -> p g u s", g=2, u=2)
                for i in range(2):
                    g = 2 * pair + i
                    for u in range(2):
                        nc.tensor.transpose(
                            flipped[:, i, u, :],
                            x_words[:, WORDS_PER_PASS * g + u : WORDS_PER_PASS * (g + 1) : 2],
                            ident[:],
                        )
                side_by_side = flipped.rearrange("p g u s -> p g s u")
                if pair == 0:
                    nc.vector.tensor_copy(out=grouped_words[:, 0:2], in_=side_by_side)
                else:
                    nc.scalar.copy(out=grouped_words[:, 2:4], in_=side_by_side)
            nc.vector.quantize_mx(
                out=x_codes[:, r, :].bitcast(FP8X4), scales=x_scales[:, r, :], in_=grouped[:]
            )


        for name, words, scales, out, n_cols, rope in weights:
            groups = [(c0, N_TILE) for c0 in range(0, n_cols, N_TILE)]
            if name == "v":
                last_c0 = groups.pop()[0]
                groups.extend([(last_c0, N_TILE // 2), (last_c0 + N_TILE // 2, N_TILE // 2)])
            for c0, width in groups:
                together = 2 if name == "q" and c0 == 0 else 1
                accs = []
                for r0 in range(0, ROW_SETS, together):
                    for r in range(r0, r0 + together):
                        acc = psum.tile([P, width], F32, tag="bank")
                        accs.append(acc)
                    tile_c0 = c0 - c0 % N_TILE
                    for g in range(K_GROUPS):
                        for r in range(r0, r0 + together):
                            nc.tensor.matmul_mx(
                                out=accs[r][:],
                                lhsT=x_codes[:, r, P * g : P * (g + 1)].bitcast(FP8X4),
                                lhsT_scale=x_scales[:, r, P * g : P * (g + 1)],
                                rhs=w_words[(name, tile_c0, g)][:, c0 - tile_c0 : c0 - tile_c0 + width].bitcast(FP8X4),
                                rhs_scale=planes[name][LIVE_ROWS * g : P, c0 : c0 + width],
                                start=(g == 0),
                                stop=(g == K_GROUPS - 1),
                            )

                h0 = c0 // HEAD
                out_rows = out[0, h0 : h0 + width // HEAD].rearrange("h (p r) d -> p h (r d)", r=ROW_SETS)
                if not rope:
                    copied = plain.tile([P, width // HEAD, ROW_SETS, HEAD], F32)
                    for r in range(ROW_SETS):
                        nc.scalar.copy(
                            out=copied[:, :, r, :], in_=accs[r][:].rearrange("p (h d) -> p h d", d=HEAD)
                        )
                    nc.scalar.dma_start(out=out_rows, in_=copied[:].rearrange("p h r d -> p h (r d)"))
                    continue

                products = roped.tile([P, 2, HEADS_PER_TILE, ROW_SETS, HEAD], F32)
                both = [P, 2, HEADS_PER_TILE, HEAD]
                for r in range(ROW_SETS):
                    by_head = accs[r][:].rearrange("p (h d) -> p h d", d=HEAD)
                    nc.vector.tensor_tensor(
                        out=products[:, :, :, r, :],
                        in0=by_head.unsqueeze(1).to_broadcast(both),
                        in1=factors[:, r].unsqueeze(2).to_broadcast(both),
                        op=MULT,
                    )
                last_rope_group = name == "k" and c0 == K_COLS - N_TILE
                first_adder = nc.vector if last_rope_group else nc.gpsimd
                second_adder = first_adder
                straight = products[:, 0].rearrange("p h r d -> p (h r) d")
                crossed = products[:, 1].rearrange("p h r d -> p (h r) d")
                first_adder.tensor_tensor(
                    out=straight[:, :, 0:HALF], in0=straight[:, :, 0:HALF], in1=crossed[:, :, HALF:HEAD], op=SUBTRACT
                )
                second_adder.tensor_tensor(
                    out=straight[:, :, HALF:HEAD], in0=straight[:, :, HALF:HEAD], in1=crossed[:, :, 0:HALF], op=ADD
                )
                nc.sync.dma_start(out=out_rows, in_=products[:, 0].rearrange("p h r d -> p h (r d)"))
